import numpy as np
import ml_dtypes


def mxq(x, axis, fmt="e4m3"):
    dtype, down = {"e4m3": (ml_dtypes.float8_e4m3fn, 7), "e5m2": (ml_dtypes.float8_e5m2, 14)}[fmt]
    v = np.moveaxis(np.asarray(x, np.float32).astype(ml_dtypes.bfloat16).astype(np.float64), axis, -1)
    blocks = v.reshape(v.shape[:-1] + (-1, 32))
    amax = np.abs(blocks).max(-1, keepdims=True)
    byte = np.maximum(np.where(amax > 0, np.frexp(amax)[1] - 1 + 127, 0) - down, 1)
    scale = np.exp2(byte - 127.0)
    codes = (blocks / scale).astype(np.float32).astype(dtype).astype(np.float64)
    return np.moveaxis((codes * scale).reshape(v.shape), -1, axis)


WIDE = False


def mx_kscale(k):
    if not WIDE:
        return np.ones(k)
    levels = np.array([10, -10, 5, -5, 0])
    a = np.random.permutation(np.resize(levels, k // 512 * 4)).reshape(k // 512, 4)
    idx = np.arange(k)
    return np.exp2(a[idx // 512, idx % 128 // 32])


BF16 = ml_dtypes.bfloat16


def bf(x):
    return np.asarray(x, np.float32).astype(BF16)


def f64(x):
    return np.asarray(x).astype(np.float64)


B, S, D, E, Q = 2, 1024, 512, 512, 512
P = S - Q


def setup_inputs():
    s = mx_kscale(E)
    return {"q_rot": bf(np.random.standard_normal((B, Q, E)) * s),
            "k_rot": bf(np.random.standard_normal((B, S, E)) / s)}


def reference(q_rot, k_rot):
    scores = (mxq(f64(q_rot), 2, "e4m3") @ mxq(f64(k_rot), 2, "e4m3").transpose(0, 2, 1)) / np.sqrt(E)
    mask = np.triu(np.full((Q, S), -np.inf), 1 + P)
    scores = scores + mask
    e = np.exp(scores - scores.max(-1, keepdims=True))
    return e / e.sum(-1, keepdims=True)

@@ -1,0 +1,208 @@
+import math
+from contextlib import ExitStack
+
+import concourse.mybir as mybir
+from concourse.masks import make_identity
+
+F32 = mybir.dt.float32
+BF16 = mybir.dt.bfloat16
+U32 = mybir.dt.uint32
+U8 = mybir.dt.uint8
+FP8X4 = mybir.dt.float8_e4m3fn_x4
+ALU = mybir.AluOpType
+ACT = mybir.ActivationFunctionType
+AXIS = mybir.AxisListType
+
+B, Q, S, E = 2, 512, 1024, 512
+P = 128
+FIRST = S - Q
+Q_TILES = Q // P
+BANK = 512
+ROWS_PER_PARTITION = 2
+PIECE = ROWS_PER_PARTITION * P
+WORDS = E // 2
+PLANES = ROWS_PER_PARTITION * WORDS // P
+SCALE = 1.0 / math.sqrt(E)
+MASKED = 1.0e30
+MX_WIDTHS = (128, 256, 512)
+
+FLOPS = 2 * B * Q * S * E
+
+PIECES = (("q", 1), ("k", 3), ("k", 2), ("k", 1), ("k", 0), ("q", 0))
+
+
+def visible_keys(m):
+    return FIRST + (m + 1) * P
+
+
+def tile_rawattention_pb_kernel(tc, q_rot, k_rot, out):
+    nc = tc.nc
+    with ExitStack() as ctx:
+        consts = ctx.enter_context(tc.tile_pool(name="consts", bufs=1))
+        loads = ctx.enter_context(tc.tile_pool(name="loads", bufs=B * len(PIECES)))
+        stage = ctx.enter_context(tc.tile_pool(name="stage", bufs=4))
+        packed = ctx.enter_context(tc.tile_pool(name="packed", bufs=B))
+        row_pool = ctx.enter_context(tc.tile_pool(name="row_pool", bufs=B * Q_TILES))
+        turn = ctx.enter_context(tc.psum_pool(name="turn", bufs=4))
+        scores = ctx.enter_context(tc.psum_pool(name="scores", bufs=2))
+
+        ident = consts.tile([P, P], F32)
+        make_identity(nc, ident[:])
+
+        beyond = consts.tile([P, BANK], F32)
+        nc.vector.memset(beyond[:], 0.0)
+        nc.gpsimd.affine_select(
+            out=beyond[:, BANK - P :],
+            in_=beyond[:, BANK - P :],
+            compare_op=ALU.is_ge,
+            fill=MASKED,
+            base=0,
+            pattern=[[-1, P]],
+            channel_multiplier=1,
+        )
+
+        zeros = consts.tile([P, S - visible_keys(0)], F32)
+        nc.vector.memset(zeros[:], 0.0)
+
+        warm = consts.tile([P, 1], F32)
+        nc.vector.memset(warm[:], 0.0)
+        nc.scalar.activation(out=warm[:], in_=warm[:], func=ACT.Exp)
+
+        upper_shift = consts.tile([P, B * Q_TILES], F32)
+        shift = consts.tile([P, B * Q_TILES], F32)
+        total = consts.tile([P, B * Q_TILES], F32)
+        inverse = consts.tile([P, B * Q_TILES], F32)
+
+        sources = {"q": q_rot, "k": k_rot}
+        raw = {}
+        for b in range(B):
+            for name, j in PIECES:
+                source_rows = sources[name][b, j * PIECE : (j + 1) * PIECE, :]
+                piece = loads.tile([P, ROWS_PER_PARTITION * E], BF16)
+                nc.sync.dma_start(
+                    out=piece[:],
+                    in_=source_rows.rearrange("(p t) e -> p (t e)", t=ROWS_PER_PARTITION),
+                )
+                raw[(b, name, j)] = piece
+
+        for b in range(B):
+            for m in range(Q_TILES - 1):
+                seen = visible_keys(m)
+                nc.sync.dma_start(
+                    out=out[b, m * P : (m + 1) * P, seen:], in_=zeros[:, : S - seen]
+                )
+
+        codes = {}
+        planes = {}
+        for b in range(B):
+            q_codes = packed.tile([P, Q], U32, align_bytes=64)
+            q_scales = packed.tile([P, Q], U8, align_bytes=64)
+            k_codes = packed.tile([P, S], U32, align_bytes=64)
+            k_scales = packed.tile([P, S], U8, align_bytes=64)
+            codes[(b, "q")], planes[(b, "q")] = q_codes, q_scales
+            codes[(b, "k")], planes[(b, "k")] = k_codes, k_scales
+
+            for name, j in PIECES:
+                words = raw[(b, name, j)][:].bitcast(F32)
+                turned = turn.tile([P, PLANES, P], F32)
+                for f in range(PLANES):
+                    nc.tensor.transpose(turned[:, f, :], words[:, f * P : (f + 1) * P], ident[:])
+                grouped = stage.tile([P, 4 * PIECE], BF16, align_bytes=64)
+                nc.scalar.copy(
+                    out=grouped[:].bitcast(F32).rearrange("w (p f) -> w p f", f=PLANES),
+                    in_=turned[:].rearrange("w f p -> w p f"),
+                )
+                cols = slice(j * PIECE, (j + 1) * PIECE)
+                nc.vector.quantize_mx(
+                    out=codes[(b, name)][:, cols].bitcast(FP8X4),
+                    scales=planes[(b, name)][:, cols],
+                    in_=grouped[:],
+                )
+
+        for b in range(B):
+            for top in range(Q_TILES - 1, 0, -2):
+                pair = (top, top - 1)
+                lower = {}
+                upper = {}
+                rows = {}
+                for m in pair:
+                    width = min(w for w in MX_WIDTHS if w >= visible_keys(m) - FIRST)
+                    upper[m] = scores.tile([P, BANK], F32, name="upper", tag="upper")
+                    nc.tensor.matmul_mx(
+                        out=upper[m][:, :width],
+                        lhsT=codes[(b, "q")][:, m * P : (m + 1) * P].bitcast(FP8X4),
+                        lhsT_scale=planes[(b, "q")][:, m * P : (m + 1) * P],
+                        rhs=codes[(b, "k")][:, FIRST : FIRST + width].bitcast(FP8X4),
+                        rhs_scale=planes[(b, "k")][:, FIRST : FIRST + width],
+                        start=True,
+                        stop=True,
+                    )
+                for m in pair:
+                    lower[m] = scores.tile([P, BANK], F32, name="lower", tag="lower")
+                    nc.tensor.matmul_mx(
+                        out=lower[m][:],
+                        lhsT=codes[(b, "q")][:, m * P : (m + 1) * P].bitcast(FP8X4),
+                        lhsT_scale=planes[(b, "q")][:, m * P : (m + 1) * P],
+                        rhs=codes[(b, "k")][:, :FIRST].bitcast(FP8X4),
+                        rhs_scale=planes[(b, "k")][:, :FIRST],
+                        start=True,
+                        stop=True,
+                    )
+
+                for m in pair:
+                    n_upper = visible_keys(m) - FIRST
+                    rows[m] = row_pool.tile([P, S], F32, name="rows", tag="rows")
+                    nc.vector.scalar_tensor_tensor(
+                        out=rows[m][:, FIRST : FIRST + n_upper],
+                        in0=upper[m][:, :n_upper],
+                        scalar=-SCALE,
+                        in1=beyond[:, BANK - n_upper :],
+                        op0=ALU.mult,
+                        op1=ALU.add,
+                    )
+                for m in pair:
+                    col = b * Q_TILES + m
+                    nc.vector.tensor_reduce(
+                        out=upper_shift[:, col : col + 1],
+                        in_=rows[m][:, FIRST : visible_keys(m)],
+                        axis=AXIS.X,
+                        op=ALU.min,
+                    )
+                for m in pair:
+                    col = b * Q_TILES + m
+                    nc.vector.tensor_scalar(
+                        out=rows[m][:, :FIRST],
+                        in0=lower[m][:],
+                        scalar1=-SCALE,
+                        scalar2=upper_shift[:, col : col + 1],
+                        op0=ALU.mult,
+                        op1=ALU.min,
+                        accum_out=shift[:, col : col + 1],
+                    )
+                for m in pair:
+                    col = b * Q_TILES + m
+                    seen = visible_keys(m)
+                    nc.scalar.activation(
+                        out=rows[m][:, :seen],
+                        in_=rows[m][:, :seen],
+                        func=ACT.Exp,
+                        scale=-1.0,
+                        bias=shift[:, col : col + 1],
+                        accum_out=total[:, col : col + 1],
+                    )
+                first_col = b * Q_TILES + pair[1]
+                nc.vector.reciprocal(
+                    out=inverse[:, first_col : first_col + 2], in_=total[:, first_col : first_col + 2]
+                )
+                for m in pair:
+                    col = b * Q_TILES + m
+                    seen = visible_keys(m)
+                    nc.gpsimd.tensor_scalar(
+                        out=rows[m][:, :seen],
+                        in0=rows[m][:, :seen],
+                        scalar1=inverse[:, col : col + 1],
+                        scalar2=0.0,
+                        op0=ALU.mult,
+                        op1=ALU.add,
+                    )
+                    nc.sync.dma_start(out=out[b, m * P : (m + 1) * P, :seen], in_=rows[m][:, :seen])

@@ -28,6 +28,10 @@ MX_WIDTHS = (128, 256, 512)
 
 FLOPS = 2 * B * Q * S * E
 
+UPPER_NEEDS = 3
+FIRST_NEEDS = 5
+PER_STEP = 2
+
 PIECES = (("q", 1), ("k", 3), ("k", 2), ("k", 1), ("k", 0), ("q", 0))
 
 
@@ -40,7 +44,7 @@ def tile_rawattention_pb_kernel(tc, q_rot, k_rot, out):
     with ExitStack() as ctx:
         consts = ctx.enter_context(tc.tile_pool(name="consts", bufs=1))
         loads = ctx.enter_context(tc.tile_pool(name="loads", bufs=B * len(PIECES)))
-        stage = ctx.enter_context(tc.tile_pool(name="stage", bufs=4))
+        stage = ctx.enter_context(tc.tile_pool(name="stage", bufs=len(PIECES)))
         packed = ctx.enter_context(tc.tile_pool(name="packed", bufs=B))
         row_pool = ctx.enter_context(tc.tile_pool(name="row_pool", bufs=B * Q_TILES))
         turn = ctx.enter_context(tc.psum_pool(name="turn", bufs=4))
@@ -74,23 +78,21 @@ def tile_rawattention_pb_kernel(tc, q_rot, k_rot, out):
         inverse = consts.tile([P, B * Q_TILES], F32)
 
         sources = {"q": q_rot, "k": k_rot}
+        pieces = [(b, name, j) for b in range(B) for name, j in PIECES]
         raw = {}
-        for b in range(B):
-            for name, j in PIECES:
-                source_rows = sources[name][b, j * PIECE : (j + 1) * PIECE, :]
-                piece = loads.tile([P, ROWS_PER_PARTITION * E], BF16)
-                nc.sync.dma_start(
-                    out=piece[:],
-                    in_=source_rows.rearrange("(p t) e -> p (t e)", t=ROWS_PER_PARTITION),
-                )
-                raw[(b, name, j)] = piece
+        for b, name, j in pieces:
+            source_rows = sources[name][b, j * PIECE : (j + 1) * PIECE, :]
+            loaded = loads.tile([P, ROWS_PER_PARTITION * E], BF16)
+            nc.sync.dma_start(
+                out=loaded[:],
+                in_=source_rows.rearrange("(p t) e -> p (t e)", t=ROWS_PER_PARTITION),
+            )
+            raw[(b, name, j)] = loaded
 
         for b in range(B):
             for m in range(Q_TILES - 1):
                 seen = visible_keys(m)
-                nc.sync.dma_start(
-                    out=out[b, m * P : (m + 1) * P, seen:], in_=zeros[:, : S - seen]
-                )
+                nc.sync.dma_start(out=out[b, m * P : (m + 1) * P, seen:], in_=zeros[:, : S - seen])
 
         codes = {}
         planes = {}
@@ -102,107 +104,127 @@ def tile_rawattention_pb_kernel(tc, q_rot, k_rot, out):
             codes[(b, "q")], planes[(b, "q")] = q_codes, q_scales
             codes[(b, "k")], planes[(b, "k")] = k_codes, k_scales
 
-            for name, j in PIECES:
-                words = raw[(b, name, j)][:].bitcast(F32)
-                turned = turn.tile([P, PLANES, P], F32)
-                for f in range(PLANES):
-                    nc.tensor.transpose(turned[:, f, :], words[:, f * P : (f + 1) * P], ident[:])
-                grouped = stage.tile([P, 4 * PIECE], BF16, align_bytes=64)
-                nc.scalar.copy(
-                    out=grouped[:].bitcast(F32).rearrange("w (p f) -> w p f", f=PLANES),
-                    in_=turned[:].rearrange("w f p -> w p f"),
-                )
-                cols = slice(j * PIECE, (j + 1) * PIECE)
-                nc.vector.quantize_mx(
-                    out=codes[(b, name)][:, cols].bitcast(FP8X4),
-                    scales=planes[(b, name)][:, cols],
-                    in_=grouped[:],
-                )
+        def prepare(piece):
+            b, name, j = piece
+            words = raw[piece][:].bitcast(F32)
+            turned = turn.tile([P, PLANES, P], F32)
+            for f in range(PLANES):
+                nc.tensor.transpose(turned[:, f, :], words[:, f * P : (f + 1) * P], ident[:])
+            grouped = stage.tile([P, 4 * PIECE], BF16, align_bytes=64)
+            nc.scalar.copy(
+                out=grouped[:].bitcast(F32).rearrange("w (p f) -> w p f", f=PLANES),
+                in_=turned[:].rearrange("w f p -> w p f"),
+            )
+            cols = slice(j * PIECE, (j + 1) * PIECE)
+            nc.vector.quantize_mx(
+                out=codes[(b, name)][:, cols].bitcast(FP8X4),
+                scales=planes[(b, name)][:, cols],
+                in_=grouped[:],
+            )
 
-        for b in range(B):
-            for top in range(Q_TILES - 1, 0, -2):
-                pair = (top, top - 1)
-                lower = {}
-                upper = {}
-                rows = {}
-                for m in pair:
-                    width = min(w for w in MX_WIDTHS if w >= visible_keys(m) - FIRST)
-                    upper[m] = scores.tile([P, BANK], F32, name="upper", tag="upper")
-                    nc.tensor.matmul_mx(
-                        out=upper[m][:, :width],
-                        lhsT=codes[(b, "q")][:, m * P : (m + 1) * P].bitcast(FP8X4),
-                        lhsT_scale=planes[(b, "q")][:, m * P : (m + 1) * P],
-                        rhs=codes[(b, "k")][:, FIRST : FIRST + width].bitcast(FP8X4),
-                        rhs_scale=planes[(b, "k")][:, FIRST : FIRST + width],
-                        start=True,
-                        stop=True,
-                    )
-                for m in pair:
-                    lower[m] = scores.tile([P, BANK], F32, name="lower", tag="lower")
-                    nc.tensor.matmul_mx(
-                        out=lower[m][:],
-                        lhsT=codes[(b, "q")][:, m * P : (m + 1) * P].bitcast(FP8X4),
-                        lhsT_scale=planes[(b, "q")][:, m * P : (m + 1) * P],
-                        rhs=codes[(b, "k")][:, :FIRST].bitcast(FP8X4),
-                        rhs_scale=planes[(b, "k")][:, :FIRST],
-                        start=True,
-                        stop=True,
-                    )
+        tiles = [(b, m) for b in range(B) for m in reversed(range(Q_TILES))]
+        upper = {}
+        lower = {}
+        rows = {}
 
-                for m in pair:
-                    n_upper = visible_keys(m) - FIRST
-                    rows[m] = row_pool.tile([P, S], F32, name="rows", tag="rows")
-                    nc.vector.scalar_tensor_tensor(
-                        out=rows[m][:, FIRST : FIRST + n_upper],
-                        in0=upper[m][:, :n_upper],
-                        scalar=-SCALE,
-                        in1=beyond[:, BANK - n_upper :],
-                        op0=ALU.mult,
-                        op1=ALU.add,
-                    )
-                for m in pair:
-                    col = b * Q_TILES + m
-                    nc.vector.tensor_reduce(
-                        out=upper_shift[:, col : col + 1],
-                        in_=rows[m][:, FIRST : visible_keys(m)],
-                        axis=AXIS.X,
-                        op=ALU.min,
-                    )
-                for m in pair:
-                    col = b * Q_TILES + m
-                    nc.vector.tensor_scalar(
-                        out=rows[m][:, :FIRST],
-                        in0=lower[m][:],
-                        scalar1=-SCALE,
-                        scalar2=upper_shift[:, col : col + 1],
-                        op0=ALU.mult,
-                        op1=ALU.min,
-                        accum_out=shift[:, col : col + 1],
-                    )
-                for m in pair:
-                    col = b * Q_TILES + m
-                    seen = visible_keys(m)
-                    nc.scalar.activation(
-                        out=rows[m][:, :seen],
-                        in_=rows[m][:, :seen],
-                        func=ACT.Exp,
-                        scale=-1.0,
-                        bias=shift[:, col : col + 1],
-                        accum_out=total[:, col : col + 1],
-                    )
-                first_col = b * Q_TILES + pair[1]
-                nc.vector.reciprocal(
-                    out=inverse[:, first_col : first_col + 2], in_=total[:, first_col : first_col + 2]
-                )
-                for m in pair:
-                    col = b * Q_TILES + m
-                    seen = visible_keys(m)
-                    nc.gpsimd.tensor_scalar(
-                        out=rows[m][:, :seen],
-                        in0=rows[m][:, :seen],
-                        scalar1=inverse[:, col : col + 1],
-                        scalar2=0.0,
-                        op0=ALU.mult,
-                        op1=ALU.add,
-                    )
-                    nc.sync.dma_start(out=out[b, m * P : (m + 1) * P, :seen], in_=rows[m][:, :seen])
+        def multiply(bank, t, first_key, width):
+            b, m = tiles[t]
+            nc.tensor.matmul_mx(
+                out=bank[:, :width],
+                lhsT=codes[(b, "q")][:, m * P : (m + 1) * P].bitcast(FP8X4),
+                lhsT_scale=planes[(b, "q")][:, m * P : (m + 1) * P],
+                rhs=codes[(b, "k")][:, first_key : first_key + width].bitcast(FP8X4),
+                rhs_scale=planes[(b, "k")][:, first_key : first_key + width],
+                start=True,
+                stop=True,
+            )
+
+        def upper_scores(t):
+            n_upper = visible_keys(tiles[t][1]) - FIRST
+            upper[t] = scores.tile([P, BANK], F32, name="upper", tag="upper")
+            multiply(upper[t], t, FIRST, min(w for w in MX_WIDTHS if w >= n_upper))
+
+        def lower_scores(t):
+            lower[t] = scores.tile([P, BANK], F32, name="lower", tag="lower")
+            multiply(lower[t], t, 0, FIRST)
+
+        def mask_upper(t):
+            n_upper = visible_keys(tiles[t][1]) - FIRST
+            rows[t] = row_pool.tile([P, S], F32, name="rows", tag="rows")
+            nc.vector.scalar_tensor_tensor(
+                out=rows[t][:, FIRST : FIRST + n_upper],
+                in0=upper[t][:, :n_upper],
+                scalar=-SCALE,
+                in1=beyond[:, BANK - n_upper :],
+                op0=ALU.mult,
+                op1=ALU.add,
+            )
+
+        def min_upper(t):
+            nc.vector.tensor_reduce(
+                out=upper_shift[:, t : t + 1],
+                in_=rows[t][:, FIRST : visible_keys(tiles[t][1])],
+                axis=AXIS.X,
+                op=ALU.min,
+            )
+
+        def min_of_row(t):
+            nc.vector.tensor_scalar(
+                out=rows[t][:, :FIRST],
+                in0=lower[t][:],
+                scalar1=-SCALE,
+                scalar2=upper_shift[:, t : t + 1],
+                op0=ALU.mult,
+                op1=ALU.min,
+                accum_out=shift[:, t : t + 1],
+            )
+
+        def exponentials(t):
+            seen = visible_keys(tiles[t][1])
+            nc.scalar.activation(
+                out=rows[t][:, :seen],
+                in_=rows[t][:, :seen],
+                func=ACT.Exp,
+                scale=-1.0,
+                bias=shift[:, t : t + 1],
+                accum_out=total[:, t : t + 1],
+            )
+
+        def normalise(t):
+            b, m = tiles[t]
+            seen = visible_keys(m)
+            nc.vector.reciprocal(out=inverse[:, t : t + 1], in_=total[:, t : t + 1])
+            nc.gpsimd.tensor_scalar(
+                out=rows[t][:, :seen],
+                in0=rows[t][:, :seen],
+                scalar1=inverse[:, t : t + 1],
+                scalar2=0.0,
+                op0=ALU.mult,
+                op1=ALU.add,
+            )
+            nc.sync.dma_start(out=out[b, m * P : (m + 1) * P, :seen], in_=rows[t][:, :seen])
+
+        for piece in pieces[:UPPER_NEEDS]:
+            prepare(piece)
+        upper_scores(0)
+        for piece in pieces[UPPER_NEEDS:FIRST_NEEDS]:
+            prepare(piece)
+        lower_scores(0)
+        mask_upper(0)
+        min_upper(0)
+        waiting = pieces[FIRST_NEEDS:]
+        for t in range(len(tiles)):
+            following = t + 1
+            if following < len(tiles):
+                upper_scores(following)
+                lower_scores(following)
+                mask_upper(following)
+            min_of_row(t)
+            exponentials(t)
+            if following < len(tiles):
+                min_upper(following)
+            if t >= 1:
+                normalise(t - 1)
+            for piece in waiting[PER_STEP * t : PER_STEP * (t + 1)]:
+                prepare(piece)
+        normalise(len(tiles) - 1)

@@ -28,23 +28,36 @@ MX_WIDTHS = (128, 256, 512)
 
 FLOPS = 2 * B * Q * S * E
 
-UPPER_NEEDS = 3
-FIRST_NEEDS = 5
-PER_STEP = 2
-
-PIECES = (("q", 1), ("k", 3), ("k", 2), ("k", 1), ("k", 0), ("q", 0))
+N_PIECES = B * (Q + S) // PIECE
+VECTOR_DIVIDES_LAST = 2
 
 
 def visible_keys(m):
     return FIRST + (m + 1) * P
 
 
+def upper_width(m):
+    return min(w for w in MX_WIDTHS if w >= visible_keys(m) - FIRST)
+
+
+def pieces_with(name, first_row, n_rows):
+    return [(name, j) for j in range(first_row // PIECE, (first_row + n_rows - 1) // PIECE + 1)]
+
+
+def upper_pieces(m):
+    return pieces_with("q", m * P, P) + pieces_with("k", FIRST, upper_width(m))
+
+
+def lower_pieces():
+    return pieces_with("k", 0, FIRST)
+
+
 def tile_rawattention_pb_kernel(tc, q_rot, k_rot, out):
     nc = tc.nc
     with ExitStack() as ctx:
         consts = ctx.enter_context(tc.tile_pool(name="consts", bufs=1))
-        loads = ctx.enter_context(tc.tile_pool(name="loads", bufs=B * len(PIECES)))
-        stage = ctx.enter_context(tc.tile_pool(name="stage", bufs=len(PIECES)))
+        loads = ctx.enter_context(tc.tile_pool(name="loads", bufs=N_PIECES))
+        stage = ctx.enter_context(tc.tile_pool(name="stage", bufs=N_PIECES // B))
         packed = ctx.enter_context(tc.tile_pool(name="packed", bufs=B))
         row_pool = ctx.enter_context(tc.tile_pool(name="row_pool", bufs=B * Q_TILES))
         turn = ctx.enter_context(tc.psum_pool(name="turn", bufs=4))
@@ -77,17 +90,22 @@ def tile_rawattention_pb_kernel(tc, q_rot, k_rot, out):
         total = consts.tile([P, B * Q_TILES], F32)
         inverse = consts.tile([P, B * Q_TILES], F32)
 
+        tiles = [
+            (b, m) for top in range(Q_TILES - 1, 0, -2) for b in range(B) for m in (top, top - 1)
+        ]
+
         sources = {"q": q_rot, "k": k_rot}
-        pieces = [(b, name, j) for b in range(B) for name, j in PIECES]
         raw = {}
-        for b, name, j in pieces:
-            source_rows = sources[name][b, j * PIECE : (j + 1) * PIECE, :]
-            loaded = loads.tile([P, ROWS_PER_PARTITION * E], BF16)
-            nc.sync.dma_start(
-                out=loaded[:],
-                in_=source_rows.rearrange("(p t) e -> p (t e)", t=ROWS_PER_PARTITION),
-            )
-            raw[(b, name, j)] = loaded
+        for b, m in tiles:
+            for name, j in upper_pieces(m) + lower_pieces():
+                if (b, name, j) not in raw:
+                    source_rows = sources[name][b, j * PIECE : (j + 1) * PIECE, :]
+                    loaded = loads.tile([P, ROWS_PER_PARTITION * E], BF16)
+                    nc.sync.dma_start(
+                        out=loaded[:],
+                        in_=source_rows.rearrange("(p t) e -> p (t e)", t=ROWS_PER_PARTITION),
+                    )
+                    raw[(b, name, j)] = loaded
 
         for b in range(B):
             for m in range(Q_TILES - 1):
@@ -104,9 +122,16 @@ def tile_rawattention_pb_kernel(tc, q_rot, k_rot, out):
             codes[(b, "q")], planes[(b, "q")] = q_codes, q_scales
             codes[(b, "k")], planes[(b, "k")] = k_codes, k_scales
 
-        def prepare(piece):
-            b, name, j = piece
-            words = raw[piece][:].bitcast(F32)
+        prepared = set()
+
+        def prepare(b, wanted):
+            for name, j in wanted:
+                if (b, name, j) not in prepared:
+                    prepared.add((b, name, j))
+                    turn_and_quantise(b, name, j)
+
+        def turn_and_quantise(b, name, j):
+            words = raw[(b, name, j)][:].bitcast(F32)
             turned = turn.tile([P, PLANES, P], F32)
             for f in range(PLANES):
                 nc.tensor.transpose(turned[:, f, :], words[:, f * P : (f + 1) * P], ident[:])
@@ -122,7 +147,6 @@ def tile_rawattention_pb_kernel(tc, q_rot, k_rot, out):
                 in_=grouped[:],
             )
 
-        tiles = [(b, m) for b in range(B) for m in reversed(range(Q_TILES))]
         upper = {}
         lower = {}
         rows = {}
@@ -140,11 +164,13 @@ def tile_rawattention_pb_kernel(tc, q_rot, k_rot, out):
             )
 
         def upper_scores(t):
-            n_upper = visible_keys(tiles[t][1]) - FIRST
+            b, m = tiles[t]
+            prepare(b, upper_pieces(m))
             upper[t] = scores.tile([P, BANK], F32, name="upper", tag="upper")
-            multiply(upper[t], t, FIRST, min(w for w in MX_WIDTHS if w >= n_upper))
+            multiply(upper[t], t, FIRST, upper_width(m))
 
         def lower_scores(t):
+            prepare(tiles[t][0], lower_pieces())
             lower[t] = scores.tile([P, BANK], F32, name="lower", tag="lower")
             multiply(lower[t], t, 0, FIRST)
 
@@ -194,25 +220,29 @@ def tile_rawattention_pb_kernel(tc, q_rot, k_rot, out):
             b, m = tiles[t]
             seen = visible_keys(m)
             nc.vector.reciprocal(out=inverse[:, t : t + 1], in_=total[:, t : t + 1])
-            nc.gpsimd.tensor_scalar(
-                out=rows[t][:, :seen],
-                in0=rows[t][:, :seen],
-                scalar1=inverse[:, t : t + 1],
-                scalar2=0.0,
-                op0=ALU.mult,
-                op1=ALU.add,
-            )
+            if t < len(tiles) - VECTOR_DIVIDES_LAST:
+                nc.gpsimd.tensor_scalar(
+                    out=rows[t][:, :seen],
+                    in0=rows[t][:, :seen],
+                    scalar1=inverse[:, t : t + 1],
+                    scalar2=0.0,
+                    op0=ALU.mult,
+                    op1=ALU.add,
+                )
+            else:
+                nc.vector.tensor_scalar(
+                    out=rows[t][:, :seen],
+                    in0=rows[t][:, :seen],
+                    scalar1=inverse[:, t : t + 1],
+                    scalar2=None,
+                    op0=ALU.mult,
+                )
             nc.sync.dma_start(out=out[b, m * P : (m + 1) * P, :seen], in_=rows[t][:, :seen])
 
-        for piece in pieces[:UPPER_NEEDS]:
-            prepare(piece)
         upper_scores(0)
-        for piece in pieces[UPPER_NEEDS:FIRST_NEEDS]:
-            prepare(piece)
         lower_scores(0)
         mask_upper(0)
         min_upper(0)
-        waiting = pieces[FIRST_NEEDS:]
         for t in range(len(tiles)):
             following = t + 1
             if following < len(tiles):
@@ -225,6 +255,4 @@ def tile_rawattention_pb_kernel(tc, q_rot, k_rot, out):
                 min_upper(following)
             if t >= 1:
                 normalise(t - 1)
-            for piece in waiting[PER_STEP * t : PER_STEP * (t + 1)]:
-                prepare(piece)
         normalise(len(tiles) - 1)

@@ -29,6 +29,7 @@ MX_WIDTHS = (128, 256, 512)
 FLOPS = 2 * B * Q * S * E
 
 N_PIECES = B * (Q + S) // PIECE
+SPLIT_FROM = 2
 VECTOR_DIVIDES_LAST = 2
 
 
@@ -85,13 +86,17 @@ def tile_rawattention_pb_kernel(tc, q_rot, k_rot, out):
         nc.vector.memset(warm[:], 0.0)
         nc.scalar.activation(out=warm[:], in_=warm[:], func=ACT.Exp)
 
+        diagonal_shift = consts.tile([P, B * Q_TILES], F32)
         upper_shift = consts.tile([P, B * Q_TILES], F32)
         shift = consts.tile([P, B * Q_TILES], F32)
         total = consts.tile([P, B * Q_TILES], F32)
         inverse = consts.tile([P, B * Q_TILES], F32)
 
         tiles = [
-            (b, m) for top in range(Q_TILES - 1, 0, -2) for b in range(B) for m in (top, top - 1)
+            (b, m)
+            for b in range(B)
+            for top in (range(1, Q_TILES, 2) if b == 0 else range(Q_TILES - 1, 0, -2))
+            for m in (top, top - 1)
         ]
 
         sources = {"q": q_rot, "k": k_rot}
@@ -174,25 +179,45 @@ def tile_rawattention_pb_kernel(tc, q_rot, k_rot, out):
             lower[t] = scores.tile([P, BANK], F32, name="lower", tag="lower")
             multiply(lower[t], t, 0, FIRST)
 
+        def open_columns(t):
+            m = tiles[t][1]
+            return m * P if m >= SPLIT_FROM else 0
+
         def mask_upper(t):
             n_upper = visible_keys(tiles[t][1]) - FIRST
+            n_open = open_columns(t)
             rows[t] = row_pool.tile([P, S], F32, name="rows", tag="rows")
             nc.vector.scalar_tensor_tensor(
-                out=rows[t][:, FIRST : FIRST + n_upper],
-                in0=upper[t][:, :n_upper],
+                out=rows[t][:, FIRST + n_open : FIRST + n_upper],
+                in0=upper[t][:, n_open:n_upper],
                 scalar=-SCALE,
-                in1=beyond[:, BANK - n_upper :],
+                in1=beyond[:, BANK - n_upper + n_open :],
                 op0=ALU.mult,
                 op1=ALU.add,
             )
 
         def min_upper(t):
+            n_open = open_columns(t)
+            masked_shift = diagonal_shift if n_open else upper_shift
             nc.vector.tensor_reduce(
-                out=upper_shift[:, t : t + 1],
-                in_=rows[t][:, FIRST : visible_keys(tiles[t][1])],
+                out=masked_shift[:, t : t + 1],
+                in_=rows[t][:, FIRST + n_open : visible_keys(tiles[t][1])],
                 axis=AXIS.X,
                 op=ALU.min,
             )
+
+        def min_open(t):
+            n_open = open_columns(t)
+            if n_open:
+                nc.vector.tensor_scalar(
+                    out=rows[t][:, FIRST : FIRST + n_open],
+                    in0=upper[t][:, :n_open],
+                    scalar1=-SCALE,
+                    scalar2=diagonal_shift[:, t : t + 1],
+                    op0=ALU.mult,
+                    op1=ALU.min,
+                    accum_out=upper_shift[:, t : t + 1],
+                )
 
         def min_of_row(t):
             nc.vector.tensor_scalar(
@@ -243,6 +268,7 @@ def tile_rawattention_pb_kernel(tc, q_rot, k_rot, out):
         lower_scores(0)
         mask_upper(0)
         min_upper(0)
+        min_open(0)
         for t in range(len(tiles)):
             following = t + 1
             if following < len(tiles):
@@ -255,4 +281,6 @@ def tile_rawattention_pb_kernel(tc, q_rot, k_rot, out):
                 min_upper(following)
             if t >= 1:
                 normalise(t - 1)
+            if following < len(tiles):
+                min_open(following)
         normalise(len(tiles) - 1)

@@ -30,6 +30,7 @@ FLOPS = 2 * B * Q * S * E
 
 N_PIECES = B * (Q + S) // PIECE
 SPLIT_FROM = 2
+WARMING = 5
 VECTOR_DIVIDES_LAST = 2
 
 
@@ -86,6 +87,12 @@ def tile_rawattention_pb_kernel(tc, q_rot, k_rot, out):
         nc.vector.memset(warm[:], 0.0)
         nc.scalar.activation(out=warm[:], in_=warm[:], func=ACT.Exp)
 
+        blank = consts.tile([P, BANK], BF16)
+        nc.vector.memset(blank[:], 0.0)
+        for i in range(WARMING):
+            unread = turn.tile([P, BANK], F32, name="turned", tag="turned")
+            nc.tensor.matmul(unread[:], lhsT=blank[:, :P], rhs=blank[:], start=True, stop=True)
+
         diagonal_shift = consts.tile([P, B * Q_TILES], F32)
         upper_shift = consts.tile([P, B * Q_TILES], F32)
         shift = consts.tile([P, B * Q_TILES], F32)
@@ -137,7 +144,7 @@ def tile_rawattention_pb_kernel(tc, q_rot, k_rot, out):
 
         def turn_and_quantise(b, name, j):
             words = raw[(b, name, j)][:].bitcast(F32)
-            turned = turn.tile([P, PLANES, P], F32)
+            turned = turn.tile([P, PLANES, P], F32, name="turned", tag="turned")
             for f in range(PLANES):
                 nc.tensor.transpose(turned[:, f, :], words[:, f * P : (f + 1) * P], ident[:])
             grouped = stage.tile([P, 4 * PIECE], BF16, align_bytes=64)

@@ -30,7 +30,8 @@ FLOPS = 2 * B * Q * S * E
 
 N_PIECES = B * (Q + S) // PIECE
 SPLIT_FROM = 2
-WARMING = 5
+WARMING = 8
+WARMING_WIDTH = 256
 VECTOR_DIVIDES_LAST = 2
 
 
@@ -65,6 +66,12 @@ def tile_rawattention_pb_kernel(tc, q_rot, k_rot, out):
         turn = ctx.enter_context(tc.psum_pool(name="turn", bufs=4))
         scores = ctx.enter_context(tc.psum_pool(name="scores", bufs=2))
 
+        blank = consts.tile([P, WARMING_WIDTH], BF16)
+        nc.gpsimd.memset(blank[:], 0.0)
+        unread = turn.tile([P, WARMING_WIDTH], F32, name="turned", tag="turned")
+        for i in range(WARMING):
+            nc.tensor.matmul(unread[:], lhsT=blank[:, :P], rhs=blank[:], start=True, stop=True)
+
         ident = consts.tile([P, P], F32)
         make_identity(nc, ident[:])
 
@@ -86,12 +93,6 @@ def tile_rawattention_pb_kernel(tc, q_rot, k_rot, out):
         warm = consts.tile([P, 1], F32)
         nc.vector.memset(warm[:], 0.0)
         nc.scalar.activation(out=warm[:], in_=warm[:], func=ACT.Exp)
-
-        blank = consts.tile([P, BANK], BF16)
-        nc.vector.memset(blank[:], 0.0)
-        for i in range(WARMING):
-            unread = turn.tile([P, BANK], F32, name="turned", tag="turned")
-            nc.tensor.matmul(unread[:], lhsT=blank[:, :P], rhs=blank[:], start=True, stop=True)
 
         diagonal_shift = consts.tile([P, B * Q_TILES], F32)
         upper_shift = consts.tile([P, B * Q_TILES], F32)

@@ -28,8 +28,7 @@ MX_WIDTHS = (128, 256, 512)
 
 FLOPS = 2 * B * Q * S * E
 
-N_PIECES = B * (Q + S) // PIECE
-SPLIT_FROM = 2
+N_PIECES = B * (Q + S) // PIECE + 1
 WARMING = 8
 WARMING_WIDTH = 256
 VECTOR_DIVIDES_LAST = 2
@@ -43,16 +42,22 @@ def upper_width(m):
     return min(w for w in MX_WIDTHS if w >= visible_keys(m) - FIRST)
 
 
-def pieces_with(name, first_row, n_rows):
-    return [(name, j) for j in range(first_row // PIECE, (first_row + n_rows - 1) // PIECE + 1)]
+def pieces_with(b, name, first_row, n_rows):
+    pieces = []
+    row = first_row
+    while row < first_row + n_rows:
+        size = P if (b, name) == (0, "q") and row < PIECE else PIECE
+        pieces.append((name, row // size * size, size))
+        row = pieces[-1][1] + size
+    return pieces
 
 
-def upper_pieces(m):
-    return pieces_with("q", m * P, P) + pieces_with("k", FIRST, upper_width(m))
+def upper_pieces(b, m):
+    return pieces_with(b, "q", m * P, P) + pieces_with(b, "k", FIRST, upper_width(m))
 
 
-def lower_pieces():
-    return pieces_with("k", 0, FIRST)
+def lower_pieces(b):
+    return pieces_with(b, "k", 0, FIRST)
 
 
 def tile_rawattention_pb_kernel(tc, q_rot, k_rot, out):
@@ -60,7 +65,7 @@ def tile_rawattention_pb_kernel(tc, q_rot, k_rot, out):
     with ExitStack() as ctx:
         consts = ctx.enter_context(tc.tile_pool(name="consts", bufs=1))
         loads = ctx.enter_context(tc.tile_pool(name="loads", bufs=N_PIECES))
-        stage = ctx.enter_context(tc.tile_pool(name="stage", bufs=N_PIECES // B))
+        stage = ctx.enter_context(tc.tile_pool(name="stage", bufs=(N_PIECES - 1) // B))
         packed = ctx.enter_context(tc.tile_pool(name="packed", bufs=B))
         row_pool = ctx.enter_context(tc.tile_pool(name="row_pool", bufs=B * Q_TILES))
         turn = ctx.enter_context(tc.psum_pool(name="turn", bufs=4))
@@ -94,7 +99,6 @@ def tile_rawattention_pb_kernel(tc, q_rot, k_rot, out):
         nc.vector.memset(warm[:], 0.0)
         nc.scalar.activation(out=warm[:], in_=warm[:], func=ACT.Exp)
 
-        diagonal_shift = consts.tile([P, B * Q_TILES], F32)
         upper_shift = consts.tile([P, B * Q_TILES], F32)
         shift = consts.tile([P, B * Q_TILES], F32)
         total = consts.tile([P, B * Q_TILES], F32)
@@ -110,15 +114,16 @@ def tile_rawattention_pb_kernel(tc, q_rot, k_rot, out):
         sources = {"q": q_rot, "k": k_rot}
         raw = {}
         for b, m in tiles:
-            for name, j in upper_pieces(m) + lower_pieces():
-                if (b, name, j) not in raw:
-                    source_rows = sources[name][b, j * PIECE : (j + 1) * PIECE, :]
-                    loaded = loads.tile([P, ROWS_PER_PARTITION * E], BF16)
+            for piece in upper_pieces(b, m) + lower_pieces(b):
+                if (b, piece) not in raw:
+                    name, start, size = piece
+                    source_rows = sources[name][b, start : start + size, :]
+                    loaded = loads.tile([P, size // P * E], BF16)
                     nc.sync.dma_start(
                         out=loaded[:],
-                        in_=source_rows.rearrange("(p t) e -> p (t e)", t=ROWS_PER_PARTITION),
+                        in_=source_rows.rearrange("(p t) e -> p (t e)", t=size // P),
                     )
-                    raw[(b, name, j)] = loaded
+                    raw[(b, piece)] = loaded
 
         for b in range(B):
             for m in range(Q_TILES - 1):
@@ -138,26 +143,28 @@ def tile_rawattention_pb_kernel(tc, q_rot, k_rot, out):
         prepared = set()
 
         def prepare(b, wanted):
-            for name, j in wanted:
-                if (b, name, j) not in prepared:
-                    prepared.add((b, name, j))
-                    turn_and_quantise(b, name, j)
+            for piece in wanted:
+                if (b, piece) not in prepared:
+                    prepared.add((b, piece))
+                    turn_and_quantise(b, piece)
 
-        def turn_and_quantise(b, name, j):
-            words = raw[(b, name, j)][:].bitcast(F32)
+        def turn_and_quantise(b, piece):
+            name, start, size = piece
+            n_planes = size // P * WORDS // P
+            words = raw[(b, piece)][:].bitcast(F32)
             turned = turn.tile([P, PLANES, P], F32, name="turned", tag="turned")
-            for f in range(PLANES):
+            for f in range(n_planes):
                 nc.tensor.transpose(turned[:, f, :], words[:, f * P : (f + 1) * P], ident[:])
             grouped = stage.tile([P, 4 * PIECE], BF16, align_bytes=64)
             nc.scalar.copy(
-                out=grouped[:].bitcast(F32).rearrange("w (p f) -> w p f", f=PLANES),
-                in_=turned[:].rearrange("w f p -> w p f"),
+                out=grouped[:, : 4 * size].bitcast(F32).rearrange("w (p f) -> w p f", f=n_planes),
+                in_=turned[:, :n_planes, :].rearrange("w f p -> w p f"),
             )
-            cols = slice(j * PIECE, (j + 1) * PIECE)
+            cols = slice(start, start + size)
             nc.vector.quantize_mx(
                 out=codes[(b, name)][:, cols].bitcast(FP8X4),
                 scales=planes[(b, name)][:, cols],
-                in_=grouped[:],
+                in_=grouped[:, : 4 * size],
             )
 
         upper = {}
@@ -178,54 +185,34 @@ def tile_rawattention_pb_kernel(tc, q_rot, k_rot, out):
 
         def upper_scores(t):
             b, m = tiles[t]
-            prepare(b, upper_pieces(m))
+            prepare(b, upper_pieces(b, m))
             upper[t] = scores.tile([P, BANK], F32, name="upper", tag="upper")
             multiply(upper[t], t, FIRST, upper_width(m))
 
         def lower_scores(t):
-            prepare(tiles[t][0], lower_pieces())
+            prepare(tiles[t][0], lower_pieces(tiles[t][0]))
             lower[t] = scores.tile([P, BANK], F32, name="lower", tag="lower")
             multiply(lower[t], t, 0, FIRST)
 
-        def open_columns(t):
-            m = tiles[t][1]
-            return m * P if m >= SPLIT_FROM else 0
-
         def mask_upper(t):
             n_upper = visible_keys(tiles[t][1]) - FIRST
-            n_open = open_columns(t)
             rows[t] = row_pool.tile([P, S], F32, name="rows", tag="rows")
             nc.vector.scalar_tensor_tensor(
-                out=rows[t][:, FIRST + n_open : FIRST + n_upper],
-                in0=upper[t][:, n_open:n_upper],
+                out=rows[t][:, FIRST : FIRST + n_upper],
+                in0=upper[t][:, :n_upper],
                 scalar=-SCALE,
-                in1=beyond[:, BANK - n_upper + n_open :],
+                in1=beyond[:, BANK - n_upper :],
                 op0=ALU.mult,
                 op1=ALU.add,
             )
 
         def min_upper(t):
-            n_open = open_columns(t)
-            masked_shift = diagonal_shift if n_open else upper_shift
             nc.vector.tensor_reduce(
-                out=masked_shift[:, t : t + 1],
-                in_=rows[t][:, FIRST + n_open : visible_keys(tiles[t][1])],
+                out=upper_shift[:, t : t + 1],
+                in_=rows[t][:, FIRST : visible_keys(tiles[t][1])],
                 axis=AXIS.X,
                 op=ALU.min,
             )
-
-        def min_open(t):
-            n_open = open_columns(t)
-            if n_open:
-                nc.vector.tensor_scalar(
-                    out=rows[t][:, FIRST : FIRST + n_open],
-                    in0=upper[t][:, :n_open],
-                    scalar1=-SCALE,
-                    scalar2=diagonal_shift[:, t : t + 1],
-                    op0=ALU.mult,
-                    op1=ALU.min,
-                    accum_out=upper_shift[:, t : t + 1],
-                )
 
         def min_of_row(t):
             nc.vector.tensor_scalar(
@@ -276,7 +263,6 @@ def tile_rawattention_pb_kernel(tc, q_rot, k_rot, out):
         lower_scores(0)
         mask_upper(0)
         min_upper(0)
-        min_open(0)
         for t in range(len(tiles)):
             following = t + 1
             if following < len(tiles):
@@ -289,6 +275,4 @@ def tile_rawattention_pb_kernel(tc, q_rot, k_rot, out):
                 min_upper(following)
             if t >= 1:
                 normalise(t - 1)
-            if following < len(tiles):
-                min_open(following)
         normalise(len(tiles) - 1)

@@ -31,6 +31,7 @@ FLOPS = 2 * B * Q * S * E
 N_PIECES = B * (Q + S) // PIECE + 1
 WARMING = 8
 WARMING_WIDTH = 256
+PIECES_A_TILE = 2
 VECTOR_DIVIDES_LAST = 2
 
 
@@ -68,8 +69,9 @@ def tile_rawattention_pb_kernel(tc, q_rot, k_rot, out):
         stage = ctx.enter_context(tc.tile_pool(name="stage", bufs=(N_PIECES - 1) // B))
         packed = ctx.enter_context(tc.tile_pool(name="packed", bufs=B))
         row_pool = ctx.enter_context(tc.tile_pool(name="row_pool", bufs=B * Q_TILES))
-        turn = ctx.enter_context(tc.psum_pool(name="turn", bufs=4))
-        scores = ctx.enter_context(tc.psum_pool(name="scores", bufs=2))
+        turn = ctx.enter_context(tc.psum_pool(name="turn", bufs=3))
+        upper_scores_pool = ctx.enter_context(tc.psum_pool(name="upper_scores_pool", bufs=2))
+        lower_scores_pool = ctx.enter_context(tc.psum_pool(name="lower_scores_pool", bufs=3))
 
         blank = consts.tile([P, WARMING_WIDTH], BF16)
         nc.gpsimd.memset(blank[:], 0.0)
@@ -100,7 +102,9 @@ def tile_rawattention_pb_kernel(tc, q_rot, k_rot, out):
         nc.scalar.activation(out=warm[:], in_=warm[:], func=ACT.Exp)
 
         upper_shift = consts.tile([P, B * Q_TILES], F32)
+        lower_max = consts.tile([P, B * Q_TILES], F32)
         shift = consts.tile([P, B * Q_TILES], F32)
+        parts = consts.tile([P, B * Q_TILES, 2], F32)
         total = consts.tile([P, B * Q_TILES], F32)
         inverse = consts.tile([P, B * Q_TILES], F32)
 
@@ -140,13 +144,18 @@ def tile_rawattention_pb_kernel(tc, q_rot, k_rot, out):
             codes[(b, "q")], planes[(b, "q")] = q_codes, q_scales
             codes[(b, "k")], planes[(b, "k")] = k_codes, k_scales
 
+        queue = list(raw)
         prepared = set()
 
-        def prepare(b, wanted):
-            for piece in wanted:
-                if (b, piece) not in prepared:
-                    prepared.add((b, piece))
-                    turn_and_quantise(b, piece)
+        def prepare(n):
+            for i in range(min(n, len(queue) - len(prepared))):
+                b, piece = queue[len(prepared)]
+                prepared.add((b, piece))
+                turn_and_quantise(b, piece)
+
+        def prepare_for(b, wanted):
+            while any((b, piece) not in prepared for piece in wanted):
+                prepare(1)
 
         def turn_and_quantise(b, piece):
             name, start, size = piece
@@ -185,13 +194,13 @@ def tile_rawattention_pb_kernel(tc, q_rot, k_rot, out):
 
         def upper_scores(t):
             b, m = tiles[t]
-            prepare(b, upper_pieces(b, m))
-            upper[t] = scores.tile([P, BANK], F32, name="upper", tag="upper")
+            prepare_for(b, upper_pieces(b, m))
+            upper[t] = upper_scores_pool.tile([P, BANK], F32, name="upper", tag="upper")
             multiply(upper[t], t, FIRST, upper_width(m))
 
         def lower_scores(t):
-            prepare(tiles[t][0], lower_pieces(tiles[t][0]))
-            lower[t] = scores.tile([P, BANK], F32, name="lower", tag="lower")
+            prepare_for(tiles[t][0], lower_pieces(tiles[t][0]))
+            lower[t] = lower_scores_pool.tile([P, BANK], F32, name="lower", tag="lower")
             multiply(lower[t], t, 0, FIRST)
 
         def mask_upper(t):
@@ -214,26 +223,39 @@ def tile_rawattention_pb_kernel(tc, q_rot, k_rot, out):
                 op=ALU.min,
             )
 
-        def min_of_row(t):
+        def max_lower(t):
+            nc.vector.tensor_reduce(
+                out=lower_max[:, t : t + 1], in_=lower[t][:], axis=AXIS.X, op=ALU.max
+            )
+
+        def shift_of_row(t):
             nc.vector.tensor_scalar(
-                out=rows[t][:, :FIRST],
-                in0=lower[t][:],
+                out=shift[:, t : t + 1],
+                in0=lower_max[:, t : t + 1],
                 scalar1=-SCALE,
                 scalar2=upper_shift[:, t : t + 1],
                 op0=ALU.mult,
                 op1=ALU.min,
-                accum_out=shift[:, t : t + 1],
             )
 
         def exponentials(t):
             seen = visible_keys(tiles[t][1])
-            nc.scalar.activation(
-                out=rows[t][:, :seen],
-                in_=rows[t][:, :seen],
-                func=ACT.Exp,
-                scale=-1.0,
-                bias=shift[:, t : t + 1],
-                accum_out=total[:, t : t + 1],
+            for half, cols, in_, scale in (
+                (0, slice(0, FIRST), lower[t][:], SCALE),
+                (1, slice(FIRST, seen), rows[t][:, FIRST:seen], -1.0),
+            ):
+                nc.scalar.activation(
+                    out=rows[t][:, cols],
+                    in_=in_,
+                    func=ACT.Exp,
+                    scale=scale,
+                    bias=shift[:, t : t + 1],
+                    accum_out=parts[:, t, half : half + 1],
+                )
+
+        def add_parts(t):
+            nc.vector.tensor_reduce(
+                out=total[:, t : t + 1], in_=parts[:, t, :], axis=AXIS.X, op=ALU.add
             )
 
         def normalise(t):
@@ -262,17 +284,24 @@ def tile_rawattention_pb_kernel(tc, q_rot, k_rot, out):
         upper_scores(0)
         lower_scores(0)
         mask_upper(0)
+        max_lower(0)
         min_upper(0)
         for t in range(len(tiles)):
             following = t + 1
+            prepare(PIECES_A_TILE)
+            shift_of_row(t)
+            exponentials(t)
             if following < len(tiles):
                 upper_scores(following)
                 lower_scores(following)
                 mask_upper(following)
-            min_of_row(t)
-            exponentials(t)
+            if t >= 1:
+                add_parts(t - 1)
             if following < len(tiles):
-                min_upper(following)
+                max_lower(following)
             if t >= 1:
                 normalise(t - 1)
+            if following < len(tiles):
+                min_upper(following)
+        add_parts(len(tiles) - 1)
         normalise(len(tiles) - 1)

@@ -31,6 +31,7 @@ FLOPS = 2 * B * Q * S * E
 N_PIECES = B * (Q + S) // PIECE + 1
 WARMING = 8
 WARMING_WIDTH = 256
+FIRST_PIECES = 6
 PIECES_A_TILE = 2
 VECTOR_DIVIDES_LAST = 2
 
@@ -66,7 +67,7 @@ def tile_rawattention_pb_kernel(tc, q_rot, k_rot, out):
     with ExitStack() as ctx:
         consts = ctx.enter_context(tc.tile_pool(name="consts", bufs=1))
         loads = ctx.enter_context(tc.tile_pool(name="loads", bufs=N_PIECES))
-        stage = ctx.enter_context(tc.tile_pool(name="stage", bufs=(N_PIECES - 1) // B))
+        stage = ctx.enter_context(tc.tile_pool(name="stage", bufs=N_PIECES))
         packed = ctx.enter_context(tc.tile_pool(name="packed", bufs=B))
         row_pool = ctx.enter_context(tc.tile_pool(name="row_pool", bufs=B * Q_TILES))
         turn = ctx.enter_context(tc.psum_pool(name="turn", bufs=3))
@@ -145,35 +146,34 @@ def tile_rawattention_pb_kernel(tc, q_rot, k_rot, out):
             codes[(b, "k")], planes[(b, "k")] = k_codes, k_scales
 
         queue = list(raw)
-        prepared = set()
+        turned = {}
+        grouped = {}
 
-        def prepare(n):
-            for i in range(min(n, len(queue) - len(prepared))):
-                b, piece = queue[len(prepared)]
-                prepared.add((b, piece))
-                turn_and_quantise(b, piece)
-
-        def prepare_for(b, wanted):
-            while any((b, piece) not in prepared for piece in wanted):
-                prepare(1)
-
-        def turn_and_quantise(b, piece):
+        def turn_piece(i):
+            b, piece = queue[i]
             name, start, size = piece
             n_planes = size // P * WORDS // P
             words = raw[(b, piece)][:].bitcast(F32)
-            turned = turn.tile([P, PLANES, P], F32, name="turned", tag="turned")
+            turned[i] = turn.tile([P, PLANES, P], F32, name="turned", tag="turned")
             for f in range(n_planes):
-                nc.tensor.transpose(turned[:, f, :], words[:, f * P : (f + 1) * P], ident[:])
-            grouped = stage.tile([P, 4 * PIECE], BF16, align_bytes=64)
+                nc.tensor.transpose(turned[i][:, f, :], words[:, f * P : (f + 1) * P], ident[:])
+
+        def copy_piece(i):
+            b, (name, start, size) = queue[i]
+            n_planes = size // P * WORDS // P
+            grouped[i] = stage.tile([P, 4 * PIECE], BF16, name="grouped", tag="grouped", align_bytes=64)
             nc.scalar.copy(
-                out=grouped[:, : 4 * size].bitcast(F32).rearrange("w (p f) -> w p f", f=n_planes),
-                in_=turned[:, :n_planes, :].rearrange("w f p -> w p f"),
+                out=grouped[i][:, : 4 * size].bitcast(F32).rearrange("w (p f) -> w p f", f=n_planes),
+                in_=turned[i][:, :n_planes, :].rearrange("w f p -> w p f"),
             )
+
+        def quantise_piece(i):
+            b, (name, start, size) = queue[i]
             cols = slice(start, start + size)
             nc.vector.quantize_mx(
                 out=codes[(b, name)][:, cols].bitcast(FP8X4),
                 scales=planes[(b, name)][:, cols],
-                in_=grouped[:, : 4 * size],
+                in_=grouped[i][:, : 4 * size],
             )
 
         upper = {}
@@ -194,12 +194,10 @@ def tile_rawattention_pb_kernel(tc, q_rot, k_rot, out):
 
         def upper_scores(t):
             b, m = tiles[t]
-            prepare_for(b, upper_pieces(b, m))
             upper[t] = upper_scores_pool.tile([P, BANK], F32, name="upper", tag="upper")
             multiply(upper[t], t, FIRST, upper_width(m))
 
         def lower_scores(t):
-            prepare_for(tiles[t][0], lower_pieces(tiles[t][0]))
             lower[t] = lower_scores_pool.tile([P, BANK], F32, name="lower", tag="lower")
             multiply(lower[t], t, 0, FIRST)
 
@@ -258,10 +256,12 @@ def tile_rawattention_pb_kernel(tc, q_rot, k_rot, out):
                 out=total[:, t : t + 1], in_=parts[:, t, :], axis=AXIS.X, op=ALU.add
             )
 
+        def invert(t):
+            nc.vector.reciprocal(out=inverse[:, t : t + 1], in_=total[:, t : t + 1])
+
         def normalise(t):
             b, m = tiles[t]
             seen = visible_keys(m)
-            nc.vector.reciprocal(out=inverse[:, t : t + 1], in_=total[:, t : t + 1])
             if t < len(tiles) - VECTOR_DIVIDES_LAST:
                 nc.gpsimd.tensor_scalar(
                     out=rows[t][:, :seen],
@@ -281,27 +281,43 @@ def tile_rawattention_pb_kernel(tc, q_rot, k_rot, out):
                 )
             nc.sync.dma_start(out=out[b, m * P : (m + 1) * P, :seen], in_=rows[t][:, :seen])
 
-        upper_scores(0)
-        lower_scores(0)
-        mask_upper(0)
-        max_lower(0)
-        min_upper(0)
-        for t in range(len(tiles)):
-            following = t + 1
-            prepare(PIECES_A_TILE)
-            shift_of_row(t)
-            exponentials(t)
-            if following < len(tiles):
-                upper_scores(following)
-                lower_scores(following)
-                mask_upper(following)
-            if t >= 1:
-                add_parts(t - 1)
-            if following < len(tiles):
-                max_lower(following)
-            if t >= 1:
-                normalise(t - 1)
-            if following < len(tiles):
-                min_upper(following)
-        add_parts(len(tiles) - 1)
-        normalise(len(tiles) - 1)
+        with tc.manual_schedule():
+            for i in range(FIRST_PIECES):
+                turn_piece(i)
+                copy_piece(i)
+                quantise_piece(i)
+            turn_piece(FIRST_PIECES)
+            copy_piece(FIRST_PIECES)
+            copied = FIRST_PIECES + 1
+            quantised = FIRST_PIECES
+            for t in range(len(tiles)):
+                upper_scores(t)
+                lower_scores(t)
+                for i in range(copied, min(copied + PIECES_A_TILE, len(queue))):
+                    turn_piece(i)
+                    copy_piece(i)
+                copied = min(copied + PIECES_A_TILE, len(queue))
+                mask_upper(t)
+                if t >= 1:
+                    shift_of_row(t - 1)
+                    exponentials(t - 1)
+                if quantised < len(queue):
+                    quantise_piece(quantised)
+                    quantised += 1
+                if t >= 2:
+                    add_parts(t - 2)
+                max_lower(t)
+                if t >= 2:
+                    invert(t - 2)
+                    normalise(t - 2)
+                min_upper(t)
+                if quantised < len(queue):
+                    quantise_piece(quantised)
+                    quantised += 1
+            last = len(tiles) - 1
+            shift_of_row(last)
+            exponentials(last)
+            for t in (last - 1, last):
+                add_parts(t)
+                invert(t)
+                normalise(t)

@@ -23,17 +23,16 @@ PIECE = ROWS_PER_PARTITION * P
 WORDS = E // 2
 PLANES = ROWS_PER_PARTITION * WORDS // P
 SCALE = 1.0 / math.sqrt(E)
-MASKED = 1.0e30
+MASKED = -1.0e30
 MX_WIDTHS = (128, 256, 512)
+OPEN_APART = 2 * P
 
 FLOPS = 2 * B * Q * S * E
 
-N_PIECES = B * (Q + S) // PIECE + 1
+N_PIECES = B * (Q + S) // PIECE
 WARMING = 8
 WARMING_WIDTH = 256
-FIRST_PIECES = 6
-PIECES_A_TILE = 2
-VECTOR_DIVIDES_LAST = 2
+VECTOR_DIVIDES_LAST = 3
 
 
 def visible_keys(m):
@@ -44,22 +43,17 @@ def upper_width(m):
     return min(w for w in MX_WIDTHS if w >= visible_keys(m) - FIRST)
 
 
-def pieces_with(b, name, first_row, n_rows):
-    pieces = []
-    row = first_row
-    while row < first_row + n_rows:
-        size = P if (b, name) == (0, "q") and row < PIECE else PIECE
-        pieces.append((name, row // size * size, size))
-        row = pieces[-1][1] + size
-    return pieces
+def pieces_with(name, first_row, n_rows):
+    start = first_row // PIECE * PIECE
+    return [(name, row) for row in range(start, first_row + n_rows, PIECE)]
 
 
-def upper_pieces(b, m):
-    return pieces_with(b, "q", m * P, P) + pieces_with(b, "k", FIRST, upper_width(m))
+def upper_pieces(m):
+    return pieces_with("q", m * P, P) + pieces_with("k", FIRST, upper_width(m))
 
 
-def lower_pieces(b):
-    return pieces_with(b, "k", 0, FIRST)
+def lower_pieces():
+    return pieces_with("k", 0, FIRST)
 
 
 def tile_rawattention_pb_kernel(tc, q_rot, k_rot, out):
@@ -102,10 +96,10 @@ def tile_rawattention_pb_kernel(tc, q_rot, k_rot, out):
         nc.vector.memset(warm[:], 0.0)
         nc.scalar.activation(out=warm[:], in_=warm[:], func=ACT.Exp)
 
-        upper_shift = consts.tile([P, B * Q_TILES], F32)
+        upper_max = consts.tile([P, B * Q_TILES], F32)
         lower_max = consts.tile([P, B * Q_TILES], F32)
         shift = consts.tile([P, B * Q_TILES], F32)
-        parts = consts.tile([P, B * Q_TILES, 2], F32)
+        parts = consts.tile([P, B * Q_TILES, 3], F32)
         total = consts.tile([P, B * Q_TILES], F32)
         inverse = consts.tile([P, B * Q_TILES], F32)
 
@@ -119,14 +113,14 @@ def tile_rawattention_pb_kernel(tc, q_rot, k_rot, out):
         sources = {"q": q_rot, "k": k_rot}
         raw = {}
         for b, m in tiles:
-            for piece in upper_pieces(b, m) + lower_pieces(b):
+            for piece in upper_pieces(m) + lower_pieces():
                 if (b, piece) not in raw:
-                    name, start, size = piece
-                    source_rows = sources[name][b, start : start + size, :]
-                    loaded = loads.tile([P, size // P * E], BF16)
+                    name, start = piece
+                    source_rows = sources[name][b, start : start + PIECE, :]
+                    loaded = loads.tile([P, ROWS_PER_PARTITION * E], BF16)
                     nc.sync.dma_start(
                         out=loaded[:],
-                        in_=source_rows.rearrange("(p t) e -> p (t e)", t=size // P),
+                        in_=source_rows.rearrange("(p t) e -> p (t e)", t=ROWS_PER_PARTITION),
                     )
                     raw[(b, piece)] = loaded
 
@@ -150,31 +144,30 @@ def tile_rawattention_pb_kernel(tc, q_rot, k_rot, out):
         grouped = {}
 
         def turn_piece(i):
-            b, piece = queue[i]
-            name, start, size = piece
-            n_planes = size // P * WORDS // P
-            words = raw[(b, piece)][:].bitcast(F32)
+            words = raw[queue[i]][:].bitcast(F32)
             turned[i] = turn.tile([P, PLANES, P], F32, name="turned", tag="turned")
-            for f in range(n_planes):
+            for f in range(PLANES):
                 nc.tensor.transpose(turned[i][:, f, :], words[:, f * P : (f + 1) * P], ident[:])
 
         def copy_piece(i):
-            b, (name, start, size) = queue[i]
-            n_planes = size // P * WORDS // P
             grouped[i] = stage.tile([P, 4 * PIECE], BF16, name="grouped", tag="grouped", align_bytes=64)
             nc.scalar.copy(
-                out=grouped[i][:, : 4 * size].bitcast(F32).rearrange("w (p f) -> w p f", f=n_planes),
-                in_=turned[i][:, :n_planes, :].rearrange("w f p -> w p f"),
+                out=grouped[i][:].bitcast(F32).rearrange("w (p f) -> w p f", f=PLANES),
+                in_=turned[i][:].rearrange("w f p -> w p f"),
             )
 
         def quantise_piece(i):
-            b, (name, start, size) = queue[i]
-            cols = slice(start, start + size)
+            b, (name, start) = queue[i]
+            cols = slice(start, start + PIECE)
             nc.vector.quantize_mx(
                 out=codes[(b, name)][:, cols].bitcast(FP8X4),
                 scales=planes[(b, name)][:, cols],
-                in_=grouped[i][:, : 4 * size],
+                in_=grouped[i][:],
             )
+
+        def last_piece_of(t):
+            b, m = tiles[t]
+            return max(queue.index((b, piece)) for piece in upper_pieces(m) + lower_pieces())
 
         upper = {}
         lower = {}
@@ -194,31 +187,48 @@ def tile_rawattention_pb_kernel(tc, q_rot, k_rot, out):
 
         def upper_scores(t):
             b, m = tiles[t]
-            upper[t] = upper_scores_pool.tile([P, BANK], F32, name="upper", tag="upper")
+            if b == 0:
+                upper[t] = upper_scores_pool.tile([P, BANK], F32, name="upper", tag="upper")[:]
+            else:
+                bank = turn.tile([P, PLANES, P], F32, name="turned", tag="turned")
+                upper[t] = bank[:].rearrange("q f k -> q (f k)")
             multiply(upper[t], t, FIRST, upper_width(m))
 
         def lower_scores(t):
             lower[t] = lower_scores_pool.tile([P, BANK], F32, name="lower", tag="lower")
             multiply(lower[t], t, 0, FIRST)
 
+        def masked_from(t):
+            open_upper = tiles[t][1] * P
+            return FIRST + (open_upper if open_upper >= OPEN_APART else 0)
+
         def mask_upper(t):
-            n_upper = visible_keys(tiles[t][1]) - FIRST
+            first, seen = masked_from(t), visible_keys(tiles[t][1])
             rows[t] = row_pool.tile([P, S], F32, name="rows", tag="rows")
-            nc.vector.scalar_tensor_tensor(
-                out=rows[t][:, FIRST : FIRST + n_upper],
-                in0=upper[t][:, :n_upper],
-                scalar=-SCALE,
-                in1=beyond[:, BANK - n_upper :],
-                op0=ALU.mult,
-                op1=ALU.add,
+            nc.vector.tensor_tensor(
+                out=rows[t][:, first:seen],
+                in0=upper[t][:, first - FIRST : seen - FIRST],
+                in1=beyond[:, BANK - (seen - first) :],
+                op=ALU.add,
             )
 
-        def min_upper(t):
+        def max_open(t):
+            first = masked_from(t)
+            if first > FIRST:
+                nc.vector.tensor_reduce(
+                    out=rows[t][:, first - 1 : first],
+                    in_=upper[t][:, : first - FIRST],
+                    axis=AXIS.X,
+                    op=ALU.max,
+                )
+
+        def max_upper(t):
+            first = masked_from(t)
             nc.vector.tensor_reduce(
-                out=upper_shift[:, t : t + 1],
-                in_=rows[t][:, FIRST : visible_keys(tiles[t][1])],
+                out=upper_max[:, t : t + 1],
+                in_=rows[t][:, first - 1 if first > FIRST else first : visible_keys(tiles[t][1])],
                 axis=AXIS.X,
-                op=ALU.min,
+                op=ALU.max,
             )
 
         def max_lower(t):
@@ -230,30 +240,32 @@ def tile_rawattention_pb_kernel(tc, q_rot, k_rot, out):
             nc.vector.tensor_scalar(
                 out=shift[:, t : t + 1],
                 in0=lower_max[:, t : t + 1],
-                scalar1=-SCALE,
-                scalar2=upper_shift[:, t : t + 1],
-                op0=ALU.mult,
-                op1=ALU.min,
+                scalar1=upper_max[:, t : t + 1],
+                scalar2=-SCALE,
+                op0=ALU.max,
+                op1=ALU.mult,
             )
 
         def exponentials(t):
-            seen = visible_keys(tiles[t][1])
-            for half, cols, in_, scale in (
-                (0, slice(0, FIRST), lower[t][:], SCALE),
-                (1, slice(FIRST, seen), rows[t][:, FIRST:seen], -1.0),
-            ):
+            first, seen = masked_from(t), visible_keys(tiles[t][1])
+            stretches = [(slice(0, FIRST), lower[t][:])]
+            if first > FIRST:
+                stretches.append((slice(FIRST, first), upper[t][:, : first - FIRST]))
+            stretches.append((slice(first, seen), rows[t][:, first:seen]))
+            for part, (cols, scores) in enumerate(stretches):
                 nc.scalar.activation(
                     out=rows[t][:, cols],
-                    in_=in_,
+                    in_=scores,
                     func=ACT.Exp,
-                    scale=scale,
+                    scale=SCALE,
                     bias=shift[:, t : t + 1],
-                    accum_out=parts[:, t, half : half + 1],
+                    accum_out=parts[:, t, part : part + 1],
                 )
 
         def add_parts(t):
+            n_parts = 3 if masked_from(t) > FIRST else 2
             nc.vector.tensor_reduce(
-                out=total[:, t : t + 1], in_=parts[:, t, :], axis=AXIS.X, op=ALU.add
+                out=total[:, t : t + 1], in_=parts[:, t, :n_parts], axis=AXIS.X, op=ALU.add
             )
 
         def invert(t):
@@ -282,42 +294,64 @@ def tile_rawattention_pb_kernel(tc, q_rot, k_rot, out):
             nc.sync.dma_start(out=out[b, m * P : (m + 1) * P, :seen], in_=rows[t][:, :seen])
 
         with tc.manual_schedule():
-            for i in range(FIRST_PIECES):
+            for i in range(4):
                 turn_piece(i)
                 copy_piece(i)
                 quantise_piece(i)
-            turn_piece(FIRST_PIECES)
-            copy_piece(FIRST_PIECES)
-            copied = FIRST_PIECES + 1
-            quantised = FIRST_PIECES
-            for t in range(len(tiles)):
+            turn_piece(4)
+            copy_piece(4)
+            for t in (0, 1):
+                upper_scores(t)
+                mask_upper(t)
+            turn_piece(5)
+            copy_piece(5)
+            quantise_piece(4)
+            max_upper(0)
+            max_upper(1)
+            turn_piece(6)
+            copy_piece(6)
+            quantise_piece(5)
+            copied = 7
+            quantised = 6
+            for t in (0, 1):
+                lower_scores(t)
+                for i in range(t + 1):
+                    turn_piece(copied)
+                    copy_piece(copied)
+                    copied += 1
+                max_lower(t)
+                quantise_piece(quantised)
+                quantised += 1
+                shift_of_row(t)
+                exponentials(t)
+            for t in range(2, len(tiles)):
                 upper_scores(t)
                 lower_scores(t)
-                for i in range(copied, min(copied + PIECES_A_TILE, len(queue))):
-                    turn_piece(i)
-                    copy_piece(i)
-                copied = min(copied + PIECES_A_TILE, len(queue))
-                mask_upper(t)
-                if t >= 1:
+                if copied < len(queue):
+                    turn_piece(copied)
+                    copy_piece(copied)
+                    copied += 1
+                if t >= 3:
+                    add_parts(t - 3)
                     shift_of_row(t - 1)
                     exponentials(t - 1)
+                mask_upper(t)
+                if t >= 3:
+                    invert(t - 3)
+                    normalise(t - 3)
+                max_open(t)
+                max_lower(t)
                 if quantised < len(queue):
                     quantise_piece(quantised)
                     quantised += 1
-                if t >= 2:
-                    add_parts(t - 2)
-                max_lower(t)
-                if t >= 2:
-                    invert(t - 2)
-                    normalise(t - 2)
-                min_upper(t)
-                if quantised < len(queue):
+                max_upper(t)
+                while t + 1 < len(tiles) and quantised <= last_piece_of(t + 1):
                     quantise_piece(quantised)
                     quantised += 1
             last = len(tiles) - 1
             shift_of_row(last)
             exponentials(last)
-            for t in (last - 1, last):
+            for t in range(len(tiles) - 3, len(tiles)):
                 add_parts(t)
                 invert(t)
                 normalise(t)

@@ -311,47 +311,53 @@ def tile_rawattention_pb_kernel(tc, q_rot, k_rot, out):
             turn_piece(6)
             copy_piece(6)
             quantise_piece(5)
-            copied = 7
-            quantised = 6
             for t in (0, 1):
                 lower_scores(t)
-                for i in range(t + 1):
-                    turn_piece(copied)
-                    copy_piece(copied)
-                    copied += 1
+                for i in range(7 + t, 8 + 2 * t):
+                    turn_piece(i)
+                    copy_piece(i)
+                if t == 1:
+                    exponentials(0)
                 max_lower(t)
-                quantise_piece(quantised)
-                quantised += 1
+                quantise_piece(6 + t)
                 shift_of_row(t)
-                exponentials(t)
+            quantised = 8
             for t in range(2, len(tiles)):
                 upper_scores(t)
                 lower_scores(t)
-                if copied < len(queue):
-                    turn_piece(copied)
-                    copy_piece(copied)
-                    copied += 1
-                if t >= 3:
-                    add_parts(t - 3)
-                    shift_of_row(t - 1)
-                    exponentials(t - 1)
-                mask_upper(t)
-                if t >= 3:
-                    invert(t - 3)
-                    normalise(t - 3)
-                max_open(t)
-                max_lower(t)
-                if quantised < len(queue):
-                    quantise_piece(quantised)
-                    quantised += 1
-                max_upper(t)
-                while t + 1 < len(tiles) and quantised <= last_piece_of(t + 1):
+                if t <= 3:
+                    turn_piece(8 + t)
+                    copy_piece(8 + t)
+                if t == 3:
+                    sums = (0, None, None, None)
+                elif t == 4:
+                    sums = (None, 1, 2, None)
+                elif t > 4:
+                    sums = (None, None, t - 2, None)
+                else:
+                    sums = (None, None, None, None)
+                for find, summed in zip((mask_upper, max_open, max_lower, max_upper), sums):
+                    if summed is not None:
+                        add_parts(summed)
+                    find(t)
+                    if summed is not None:
+                        invert(summed)
+                        if summed < len(tiles) - VECTOR_DIVIDES_LAST:
+                            normalise(summed)
+                    if find is mask_upper:
+                        if t > 2:
+                            shift_of_row(t - 1)
+                        exponentials(t - 1)
+                        if t == 4:
+                            quantise_piece(11)
+                while t < 4 and quantised < 7 + 2 * (t - 1):
                     quantise_piece(quantised)
                     quantised += 1
             last = len(tiles) - 1
             shift_of_row(last)
             exponentials(last)
-            for t in range(len(tiles) - 3, len(tiles)):
+            normalise(last - 2)
+            for t in (last - 1, last):
                 add_parts(t)
                 invert(t)
                 normalise(t)

@@ -33,6 +33,7 @@ N_PIECES = B * (Q + S) // PIECE
 WARMING = 8
 WARMING_WIDTH = 256
 VECTOR_DIVIDES_LAST = 3
+STORED_IN_TWO = (4,)
 
 
 def visible_keys(m):
@@ -274,24 +275,28 @@ def tile_rawattention_pb_kernel(tc, q_rot, k_rot, out):
         def normalise(t):
             b, m = tiles[t]
             seen = visible_keys(m)
-            if t < len(tiles) - VECTOR_DIVIDES_LAST:
-                nc.gpsimd.tensor_scalar(
-                    out=rows[t][:, :seen],
-                    in0=rows[t][:, :seen],
-                    scalar1=inverse[:, t : t + 1],
-                    scalar2=0.0,
-                    op0=ALU.mult,
-                    op1=ALU.add,
+            stretches = ((0, FIRST), (FIRST, seen)) if t in STORED_IN_TWO else ((0, seen),)
+            for first, end in stretches:
+                if t < len(tiles) - VECTOR_DIVIDES_LAST:
+                    nc.gpsimd.tensor_scalar(
+                        out=rows[t][:, first:end],
+                        in0=rows[t][:, first:end],
+                        scalar1=inverse[:, t : t + 1],
+                        scalar2=0.0,
+                        op0=ALU.mult,
+                        op1=ALU.add,
+                    )
+                else:
+                    nc.vector.tensor_scalar(
+                        out=rows[t][:, first:end],
+                        in0=rows[t][:, first:end],
+                        scalar1=inverse[:, t : t + 1],
+                        scalar2=None,
+                        op0=ALU.mult,
+                    )
+                nc.sync.dma_start(
+                    out=out[b, m * P : (m + 1) * P, first:end], in_=rows[t][:, first:end]
                 )
-            else:
-                nc.vector.tensor_scalar(
-                    out=rows[t][:, :seen],
-                    in0=rows[t][:, :seen],
-                    scalar1=inverse[:, t : t + 1],
-                    scalar2=None,
-                    op0=ALU.mult,
-                )
-            nc.sync.dma_start(out=out[b, m * P : (m + 1) * P, :seen], in_=rows[t][:, :seen])
 
         with tc.manual_schedule():
             for i in range(4):
@@ -333,7 +338,7 @@ def tile_rawattention_pb_kernel(tc, q_rot, k_rot, out):
                 elif t == 4:
                     sums = (None, 1, 2, None)
                 elif t > 4:
-                    sums = (None, None, t - 2, None)
+                    sums = (None, None, None, t - 2)
                 else:
                     sums = (None, None, None, None)
                 for find, summed in zip((mask_upper, max_open, max_lower, max_upper), sums):
@@ -348,16 +353,16 @@ def tile_rawattention_pb_kernel(tc, q_rot, k_rot, out):
                         if t > 2:
                             shift_of_row(t - 1)
                         exponentials(t - 1)
-                        if t == 4:
-                            quantise_piece(11)
-                while t < 4 and quantised < 7 + 2 * (t - 1):
+                while t < 4 and quantised < (9, 12)[t - 2]:
                     quantise_piece(quantised)
                     quantised += 1
             last = len(tiles) - 1
             shift_of_row(last)
             exponentials(last)
+            add_parts(last - 1)
             normalise(last - 2)
-            for t in (last - 1, last):
-                add_parts(t)
-                invert(t)
-                normalise(t)
+            invert(last - 1)
+            add_parts(last)
+            normalise(last - 1)
+            invert(last)
+            normalise(last)

@@ -32,8 +32,7 @@ FLOPS = 2 * B * Q * S * E
 N_PIECES = B * (Q + S) // PIECE
 WARMING = 8
 WARMING_WIDTH = 256
-VECTOR_DIVIDES_LAST = 3
-STORED_IN_TWO = (4,)
+VECTOR_DIVIDES_LAST = 4
 
 
 def visible_keys(m):
@@ -275,28 +274,24 @@ def tile_rawattention_pb_kernel(tc, q_rot, k_rot, out):
         def normalise(t):
             b, m = tiles[t]
             seen = visible_keys(m)
-            stretches = ((0, FIRST), (FIRST, seen)) if t in STORED_IN_TWO else ((0, seen),)
-            for first, end in stretches:
-                if t < len(tiles) - VECTOR_DIVIDES_LAST:
-                    nc.gpsimd.tensor_scalar(
-                        out=rows[t][:, first:end],
-                        in0=rows[t][:, first:end],
-                        scalar1=inverse[:, t : t + 1],
-                        scalar2=0.0,
-                        op0=ALU.mult,
-                        op1=ALU.add,
-                    )
-                else:
-                    nc.vector.tensor_scalar(
-                        out=rows[t][:, first:end],
-                        in0=rows[t][:, first:end],
-                        scalar1=inverse[:, t : t + 1],
-                        scalar2=None,
-                        op0=ALU.mult,
-                    )
-                nc.sync.dma_start(
-                    out=out[b, m * P : (m + 1) * P, first:end], in_=rows[t][:, first:end]
+            if t < len(tiles) - VECTOR_DIVIDES_LAST:
+                nc.gpsimd.tensor_scalar(
+                    out=rows[t][:, :seen],
+                    in0=rows[t][:, :seen],
+                    scalar1=inverse[:, t : t + 1],
+                    scalar2=0.0,
+                    op0=ALU.mult,
+                    op1=ALU.add,
                 )
+            else:
+                nc.vector.tensor_scalar(
+                    out=rows[t][:, :seen],
+                    in0=rows[t][:, :seen],
+                    scalar1=inverse[:, t : t + 1],
+                    scalar2=None,
+                    op0=ALU.mult,
+                )
+            nc.sync.dma_start(out=out[b, m * P : (m + 1) * P, :seen], in_=rows[t][:, :seen])
 
         with tc.manual_schedule():
             for i in range(4):
@@ -313,56 +308,59 @@ def tile_rawattention_pb_kernel(tc, q_rot, k_rot, out):
             quantise_piece(4)
             max_upper(0)
             max_upper(1)
-            turn_piece(6)
-            copy_piece(6)
+            lower_scores(0)
+            for i in (6, 7):
+                turn_piece(i)
+                copy_piece(i)
+            max_lower(0)
             quantise_piece(5)
-            for t in (0, 1):
-                lower_scores(t)
-                for i in range(7 + t, 8 + 2 * t):
-                    turn_piece(i)
-                    copy_piece(i)
-                if t == 1:
-                    exponentials(0)
-                max_lower(t)
-                quantise_piece(6 + t)
-                shift_of_row(t)
-            quantised = 8
+            shift_of_row(0)
+            exponentials(0)
+            lower_scores(1)
+            max_lower(1)
+            quantise_piece(6)
+            shift_of_row(1)
+            quantise_piece(7)
             for t in range(2, len(tiles)):
                 upper_scores(t)
                 lower_scores(t)
-                if t <= 3:
-                    turn_piece(8 + t)
-                    copy_piece(8 + t)
-                if t == 3:
-                    sums = (0, None, None, None)
-                elif t == 4:
-                    sums = (None, 1, 2, None)
-                elif t > 4:
-                    sums = (None, None, None, t - 2)
+                if t == 2:
+                    turn_piece(8)
+                    copy_piece(8)
+                    exponentials(1)
+                    turn_piece(9)
+                    copy_piece(9)
+                elif t == 3:
+                    for i in (10, 11):
+                        turn_piece(i)
+                        copy_piece(i)
+                mask_upper(t)
+                if t >= 3:
+                    shift_of_row(t - 1)
+                    exponentials(t - 1)
+                max_open(t)
+                if t >= 4:
+                    add_parts(t - 2)
+                max_lower(t)
+                if t >= 4:
+                    invert(t - 2)
                 else:
-                    sums = (None, None, None, None)
-                for find, summed in zip((mask_upper, max_open, max_lower, max_upper), sums):
-                    if summed is not None:
-                        add_parts(summed)
-                    find(t)
-                    if summed is not None:
-                        invert(summed)
-                        if summed < len(tiles) - VECTOR_DIVIDES_LAST:
-                            normalise(summed)
-                    if find is mask_upper:
-                        if t > 2:
-                            shift_of_row(t - 1)
-                        exponentials(t - 1)
-                while t < 4 and quantised < (9, 12)[t - 2]:
-                    quantise_piece(quantised)
-                    quantised += 1
+                    add_parts(t - 2)
+                max_upper(t)
+                if t == 3:
+                    for i in (9, 10, 11):
+                        quantise_piece(i)
+                if t < 4:
+                    invert(t - 2)
+                if t < 7:
+                    normalise(t - 2)
+                if t == 2:
+                    quantise_piece(8)
             last = len(tiles) - 1
             shift_of_row(last)
             exponentials(last)
-            add_parts(last - 1)
             normalise(last - 2)
-            invert(last - 1)
-            add_parts(last)
-            normalise(last - 1)
-            invert(last)
-            normalise(last)
+            for t in (last - 1, last):
+                add_parts(t)
+                invert(t)
+                normalise(t)

@@ -30,8 +30,10 @@ OPEN_APART = 2 * P
 FLOPS = 2 * B * Q * S * E
 
 N_PIECES = B * (Q + S) // PIECE
-WARMING = 8
+WARMING = 4
 WARMING_WIDTH = 256
+WARMED_BY_ZEROS = (1, 2, 3, 4)
+WARMED_BY_SCORES = (5,)
 VECTOR_DIVIDES_LAST = 4
 
 
@@ -68,11 +70,11 @@ def tile_rawattention_pb_kernel(tc, q_rot, k_rot, out):
         upper_scores_pool = ctx.enter_context(tc.psum_pool(name="upper_scores_pool", bufs=2))
         lower_scores_pool = ctx.enter_context(tc.psum_pool(name="lower_scores_pool", bufs=3))
 
-        blank = consts.tile([P, WARMING_WIDTH], BF16)
+        blank = consts.tile([P, BANK], BF16)
         nc.gpsimd.memset(blank[:], 0.0)
         unread = turn.tile([P, WARMING_WIDTH], F32, name="turned", tag="turned")
         for i in range(WARMING):
-            nc.tensor.matmul(unread[:], lhsT=blank[:, :P], rhs=blank[:], start=True, stop=True)
+            nc.tensor.matmul(unread[:], lhsT=blank[:, :P], rhs=blank[:, :WARMING_WIDTH], start=True, stop=True)
 
         ident = consts.tile([P, P], F32)
         make_identity(nc, ident[:])
@@ -146,6 +148,11 @@ def tile_rawattention_pb_kernel(tc, q_rot, k_rot, out):
         def turn_piece(i):
             words = raw[queue[i]][:].bitcast(F32)
             turned[i] = turn.tile([P, PLANES, P], F32, name="turned", tag="turned")
+            bank = turned[i][:].rearrange("w f p -> w (f p)")
+            if i in WARMED_BY_ZEROS:
+                nc.tensor.matmul(bank, lhsT=blank[:, :P], rhs=blank[:], start=True, stop=True)
+            elif i in WARMED_BY_SCORES:
+                multiply(bank, 0, FIRST, PIECE)
             for f in range(PLANES):
                 nc.tensor.transpose(turned[i][:, f, :], words[:, f * P : (f + 1) * P], ident[:])
 

import math
from contextlib import ExitStack

import concourse.mybir as mybir
from concourse.masks import make_identity

F32 = mybir.dt.float32
BF16 = mybir.dt.bfloat16
U32 = mybir.dt.uint32
U8 = mybir.dt.uint8
FP8X4 = mybir.dt.float8_e4m3fn_x4
ALU = mybir.AluOpType
ACT = mybir.ActivationFunctionType
AXIS = mybir.AxisListType

B, Q, S, E = 2, 512, 1024, 512
P = 128
FIRST = S - Q
Q_TILES = Q // P
BANK = 512
ROWS_PER_PARTITION = 2
PIECE = ROWS_PER_PARTITION * P
WORDS = E // 2
PLANES = ROWS_PER_PARTITION * WORDS // P
SCALE = 1.0 / math.sqrt(E)
MASKED = -1.0e30
MX_WIDTHS = (128, 256, 512)
OPEN_APART = 2 * P

FLOPS = 2 * B * Q * S * E

N_PIECES = B * (Q + S) // PIECE
WARMING = 4
WARMING_WIDTH = 256
WARMED_BY_ZEROS = (1, 2, 3, 4)
WARMED_BY_SCORES = (5,)
VECTOR_DIVIDES_LAST = 4


def visible_keys(m):
    return FIRST + (m + 1) * P


def upper_width(m):
    return min(w for w in MX_WIDTHS if w >= visible_keys(m) - FIRST)


def pieces_with(name, first_row, n_rows):
    start = first_row // PIECE * PIECE
    return [(name, row) for row in range(start, first_row + n_rows, PIECE)]


def upper_pieces(m):
    return pieces_with("q", m * P, P) + pieces_with("k", FIRST, upper_width(m))


def lower_pieces():
    return pieces_with("k", 0, FIRST)


def tile_rawattention_pb_kernel(tc, q_rot, k_rot, out):
    nc = tc.nc
    with ExitStack() as ctx:
        consts = ctx.enter_context(tc.tile_pool(name="consts", bufs=1))
        loads = ctx.enter_context(tc.tile_pool(name="loads", bufs=N_PIECES))
        stage = ctx.enter_context(tc.tile_pool(name="stage", bufs=N_PIECES))
        packed = ctx.enter_context(tc.tile_pool(name="packed", bufs=B))
        row_pool = ctx.enter_context(tc.tile_pool(name="row_pool", bufs=B * Q_TILES))
        turn = ctx.enter_context(tc.psum_pool(name="turn", bufs=3))
        upper_scores_pool = ctx.enter_context(tc.psum_pool(name="upper_scores_pool", bufs=2))
        lower_scores_pool = ctx.enter_context(tc.psum_pool(name="lower_scores_pool", bufs=3))

        blank = consts.tile([P, BANK], BF16)
        nc.gpsimd.memset(blank[:], 0.0)
        unread = turn.tile([P, WARMING_WIDTH], F32, name="turned", tag="turned")
        for i in range(WARMING):
            nc.tensor.matmul(unread[:], lhsT=blank[:, :P], rhs=blank[:, :WARMING_WIDTH], start=True, stop=True)

        ident = consts.tile([P, P], F32)
        make_identity(nc, ident[:])

        beyond = consts.tile([P, BANK], F32)
        nc.vector.memset(beyond[:], 0.0)
        nc.gpsimd.affine_select(
            out=beyond[:, BANK - P :],
            in_=beyond[:, BANK - P :],
            compare_op=ALU.is_ge,
            fill=MASKED,
            base=0,
            pattern=[[-1, P]],
            channel_multiplier=1,
        )

        zeros = consts.tile([P, S - visible_keys(0)], F32)
        nc.vector.memset(zeros[:], 0.0)

        warm = consts.tile([P, 1], F32)
        nc.vector.memset(warm[:], 0.0)
        nc.scalar.activation(out=warm[:], in_=warm[:], func=ACT.Exp)

        upper_max = consts.tile([P, B * Q_TILES], F32)
        lower_max = consts.tile([P, B * Q_TILES], F32)
        shift = consts.tile([P, B * Q_TILES], F32)
        parts = consts.tile([P, B * Q_TILES, 3], F32)
        total = consts.tile([P, B * Q_TILES], F32)
        inverse = consts.tile([P, B * Q_TILES], F32)

        tiles = [
            (b, m)
            for b in range(B)
            for top in (range(1, Q_TILES, 2) if b == 0 else range(Q_TILES - 1, 0, -2))
            for m in (top, top - 1)
        ]

        sources = {"q": q_rot, "k": k_rot}
        raw = {}
        for b, m in tiles:
            for piece in upper_pieces(m) + lower_pieces():
                if (b, piece) not in raw:
                    name, start = piece
                    source_rows = sources[name][b, start : start + PIECE, :]
                    loaded = loads.tile([P, ROWS_PER_PARTITION * E], BF16)
                    nc.sync.dma_start(
                        out=loaded[:],
                        in_=source_rows.rearrange("(p t) e -> p (t e)", t=ROWS_PER_PARTITION),
                    )
                    raw[(b, piece)] = loaded

        for b in range(B):
            for m in range(Q_TILES - 1):
                seen = visible_keys(m)
                nc.sync.dma_start(out=out[b, m * P : (m + 1) * P, seen:], in_=zeros[:, : S - seen])

        codes = {}
        planes = {}
        for b in range(B):
            q_codes = packed.tile([P, Q], U32, align_bytes=64)
            q_scales = packed.tile([P, Q], U8, align_bytes=64)
            k_codes = packed.tile([P, S], U32, align_bytes=64)
            k_scales = packed.tile([P, S], U8, align_bytes=64)
            codes[(b, "q")], planes[(b, "q")] = q_codes, q_scales
            codes[(b, "k")], planes[(b, "k")] = k_codes, k_scales

        queue = list(raw)
        turned = {}
        grouped = {}

        def turn_piece(i):
            words = raw[queue[i]][:].bitcast(F32)
            turned[i] = turn.tile([P, PLANES, P], F32, name="turned", tag="turned")
            bank = turned[i][:].rearrange("w f p -> w (f p)")
            if i in WARMED_BY_ZEROS:
                nc.tensor.matmul(bank, lhsT=blank[:, :P], rhs=blank[:], start=True, stop=True)
            elif i in WARMED_BY_SCORES:
                multiply(bank, 0, FIRST, PIECE)
            for f in range(PLANES):
                nc.tensor.transpose(turned[i][:, f, :], words[:, f * P : (f + 1) * P], ident[:])

        def copy_piece(i):
            grouped[i] = stage.tile([P, 4 * PIECE], BF16, name="grouped", tag="grouped", align_bytes=64)
            nc.scalar.copy(
                out=grouped[i][:].bitcast(F32).rearrange("w (p f) -> w p f", f=PLANES),
                in_=turned[i][:].rearrange("w f p -> w p f"),
            )

        def quantise_piece(i):
            b, (name, start) = queue[i]
            cols = slice(start, start + PIECE)
            nc.vector.quantize_mx(
                out=codes[(b, name)][:, cols].bitcast(FP8X4),
                scales=planes[(b, name)][:, cols],
                in_=grouped[i][:],
            )

        def last_piece_of(t):
            b, m = tiles[t]
            return max(queue.index((b, piece)) for piece in upper_pieces(m) + lower_pieces())

        upper = {}
        lower = {}
        rows = {}

        def multiply(bank, t, first_key, width):
            b, m = tiles[t]
            nc.tensor.matmul_mx(
                out=bank[:, :width],
                lhsT=codes[(b, "q")][:, m * P : (m + 1) * P].bitcast(FP8X4),
                lhsT_scale=planes[(b, "q")][:, m * P : (m + 1) * P],
                rhs=codes[(b, "k")][:, first_key : first_key + width].bitcast(FP8X4),
                rhs_scale=planes[(b, "k")][:, first_key : first_key + width],
                start=True,
                stop=True,
            )

        def upper_scores(t):
            b, m = tiles[t]
            if b == 0:
                upper[t] = upper_scores_pool.tile([P, BANK], F32, name="upper", tag="upper")[:]
            else:
                bank = turn.tile([P, PLANES, P], F32, name="turned", tag="turned")
                upper[t] = bank[:].rearrange("q f k -> q (f k)")
            multiply(upper[t], t, FIRST, upper_width(m))

        def lower_scores(t):
            lower[t] = lower_scores_pool.tile([P, BANK], F32, name="lower", tag="lower")
            multiply(lower[t], t, 0, FIRST)

        def masked_from(t):
            open_upper = tiles[t][1] * P
            return FIRST + (open_upper if open_upper >= OPEN_APART else 0)

        def mask_upper(t):
            first, seen = masked_from(t), visible_keys(tiles[t][1])
            rows[t] = row_pool.tile([P, S], F32, name="rows", tag="rows")
            nc.vector.tensor_tensor(
                out=rows[t][:, first:seen],
                in0=upper[t][:, first - FIRST : seen - FIRST],
                in1=beyond[:, BANK - (seen - first) :],
                op=ALU.add,
            )

        def max_open(t):
            first = masked_from(t)
            if first > FIRST:
                nc.vector.tensor_reduce(
                    out=rows[t][:, first - 1 : first],
                    in_=upper[t][:, : first - FIRST],
                    axis=AXIS.X,
                    op=ALU.max,
                )

        def max_upper(t):
            first = masked_from(t)
            nc.vector.tensor_reduce(
                out=upper_max[:, t : t + 1],
                in_=rows[t][:, first - 1 if first > FIRST else first : visible_keys(tiles[t][1])],
                axis=AXIS.X,
                op=ALU.max,
            )

        def max_lower(t):
            nc.vector.tensor_reduce(
                out=lower_max[:, t : t + 1], in_=lower[t][:], axis=AXIS.X, op=ALU.max
            )

        def shift_of_row(t):
            nc.vector.tensor_scalar(
                out=shift[:, t : t + 1],
                in0=lower_max[:, t : t + 1],
                scalar1=upper_max[:, t : t + 1],
                scalar2=-SCALE,
                op0=ALU.max,
                op1=ALU.mult,
            )

        def exponentials(t):
            first, seen = masked_from(t), visible_keys(tiles[t][1])
            stretches = [(slice(0, FIRST), lower[t][:])]
            if first > FIRST:
                stretches.append((slice(FIRST, first), upper[t][:, : first - FIRST]))
            stretches.append((slice(first, seen), rows[t][:, first:seen]))
            for part, (cols, scores) in enumerate(stretches):
                nc.scalar.activation(
                    out=rows[t][:, cols],
                    in_=scores,
                    func=ACT.Exp,
                    scale=SCALE,
                    bias=shift[:, t : t + 1],
                    accum_out=parts[:, t, part : part + 1],
                )

        def add_parts(t):
            n_parts = 3 if masked_from(t) > FIRST else 2
            nc.vector.tensor_reduce(
                out=total[:, t : t + 1], in_=parts[:, t, :n_parts], axis=AXIS.X, op=ALU.add
            )

        def invert(t):
            nc.vector.reciprocal(out=inverse[:, t : t + 1], in_=total[:, t : t + 1])

        def normalise(t):
            b, m = tiles[t]
            seen = visible_keys(m)
            if t < len(tiles) - VECTOR_DIVIDES_LAST:
                nc.gpsimd.tensor_scalar(
                    out=rows[t][:, :seen],
                    in0=rows[t][:, :seen],
                    scalar1=inverse[:, t : t + 1],
                    scalar2=0.0,
                    op0=ALU.mult,
                    op1=ALU.add,
                )
            else:
                nc.vector.tensor_scalar(
                    out=rows[t][:, :seen],
                    in0=rows[t][:, :seen],
                    scalar1=inverse[:, t : t + 1],
                    scalar2=None,
                    op0=ALU.mult,
                )
            nc.sync.dma_start(out=out[b, m * P : (m + 1) * P, :seen], in_=rows[t][:, :seen])

        with tc.manual_schedule():
            for i in range(4):
                turn_piece(i)
                copy_piece(i)
                quantise_piece(i)
            turn_piece(4)
            copy_piece(4)
            for t in (0, 1):
                upper_scores(t)
                mask_upper(t)
            turn_piece(5)
            copy_piece(5)
            quantise_piece(4)
            max_upper(0)
            max_upper(1)
            lower_scores(0)
            for i in (6, 7):
                turn_piece(i)
                copy_piece(i)
            max_lower(0)
            quantise_piece(5)
            shift_of_row(0)
            exponentials(0)
            lower_scores(1)
            max_lower(1)
            quantise_piece(6)
            shift_of_row(1)
            quantise_piece(7)
            for t in range(2, len(tiles)):
                upper_scores(t)
                lower_scores(t)
                if t == 2:
                    turn_piece(8)
                    copy_piece(8)
                    exponentials(1)
                    turn_piece(9)
                    copy_piece(9)
                elif t == 3:
                    for i in (10, 11):
                        turn_piece(i)
                        copy_piece(i)
                mask_upper(t)
                if t >= 3:
                    shift_of_row(t - 1)
                    exponentials(t - 1)
                max_open(t)
                if t >= 4:
                    add_parts(t - 2)
                max_lower(t)
                if t >= 4:
                    invert(t - 2)
                else:
                    add_parts(t - 2)
                max_upper(t)
                if t == 3:
                    for i in (9, 10, 11):
                        quantise_piece(i)
                if t < 4:
                    invert(t - 2)
                if t < 7:
                    normalise(t - 2)
                if t == 2:
                    quantise_piece(8)
            last = len(tiles) - 1
            shift_of_row(last)
            exponentials(last)
            normalise(last - 2)
            for t in (last - 1, last):
                add_parts(t)
                invert(t)
                normalise(t)
